import numpy as np
import ml_dtypes


def mxq(x, axis, fmt="e4m3"):
    dtype, down = {"e4m3": (ml_dtypes.float8_e4m3fn, 7), "e5m2": (ml_dtypes.float8_e5m2, 14)}[fmt]
    v = np.moveaxis(np.asarray(x, np.float32).astype(ml_dtypes.bfloat16).astype(np.float64), axis, -1)
    blocks = v.reshape(v.shape[:-1] + (-1, 32))
    amax = np.abs(blocks).max(-1, keepdims=True)
    byte = np.maximum(np.where(amax > 0, np.frexp(amax)[1] - 1 + 127, 0) - down, 1)
    scale = np.exp2(byte - 127.0)
    codes = (blocks / scale).astype(np.float32).astype(dtype).astype(np.float64)
    return np.moveaxis((codes * scale).reshape(v.shape), -1, axis)


WIDE = False


def mx_kscale(k):
    if not WIDE:
        return np.ones(k)
    levels = np.array([10, -10, 5, -5, 0])
    if k % 512:
        return np.exp2(np.random.permutation(np.resize(levels, k // 32))).repeat(32)
    a = np.empty((k // 512, 16))
    for p in range(k // 512):
        a[p, :8] = np.random.permutation(np.resize(levels, 8))
        for g in range(8):
            far = levels[np.abs(levels - a[p, g]) >= 10]
            a[p, g + 8] = far[np.random.randint(len(far))]
    return np.exp2(a.ravel()).repeat(32)


BF16 = ml_dtypes.bfloat16


def bf(x):
    return np.asarray(x, np.float32).astype(BF16)


def f64(x):
    return np.asarray(x).astype(np.float64)


B, N, D, H, DK, DV = 4, 1024, 512, 8, 64, 64


def xnorm(x, g):
    n = np.sqrt(np.sum(x * x, axis=-1, keepdims=True))
    return x * g / n


def draw0():
    s = mx_kscale(D)
    return {
        "queries": bf(np.random.standard_normal((B, N, D)) * s),
        "Wq": bf(np.random.standard_normal((D, H * DK)) / np.sqrt(D) / s[:, None]),
        "bq": bf(np.random.standard_normal(H * DK) * 0.1),
        "gamma": bf(np.random.standard_normal((1, H, 1, 1)) * 2.0),
    }


def core(queries, Wq, bq, gamma):
    q = ((mxq(f64(queries), 2, "e4m3") @ mxq(f64(Wq), 0, "e4m3")) + f64(bq)).reshape(B, N, H, DK)
    return xnorm(q.transpose(0, 2, 1, 3), f64(gamma))


def e4m3fn_bytes(y):
    return np.clip(np.asarray(y, np.float64), -448.0, 448.0).astype(np.float32).astype(ml_dtypes.float8_e4m3fn).view(np.uint8)


def e4m3fn_values(b):
    return np.asarray(b, np.uint8).view(ml_dtypes.float8_e4m3fn).astype(np.float64)


def setup_inputs():
    d = draw0()
    x0 = np.asarray(d['queries']).astype(np.float64)
    s = (np.max(np.abs(x0), axis=(0, 1), keepdims=True) / 448.0).astype(np.float32)
    out = {}
    for k, v in d.items():
        if k == 'queries':
            out['queries_bytes'] = e4m3fn_bytes(x0 / s.astype(np.float64))
            out['queries_scale'] = s
        else:
            out[k] = v
    return out


def reference(queries_bytes, queries_scale, Wq, bq, gamma):
    return core(e4m3fn_values(queries_bytes) * queries_scale.astype(np.float64), Wq, bq, gamma)

@@ -1,0 +1,290 @@
+from contextlib import ExitStack
+
+import concourse.mybir as mybir
+from concourse.masks import make_identity
+
+B, N, D, H, DK = 4, 1024, 512, 8, 64
+FLOPS = 2 * B * N * D * H * DK
+
+F32 = mybir.dt.float32
+BF16 = mybir.dt.bfloat16
+U32 = mybir.dt.uint32
+U8 = mybir.dt.uint8
+FP8 = mybir.dt.float8_e4m3fn
+FP8X4 = mybir.dt.float8_e4m3fn_x4
+ALU = mybir.AluOpType
+ACT = mybir.ActivationFunctionType
+
+P = 128
+TPB = N // P
+SMAX = 4
+SIZES = [[1,1,2,2,2],[4,4],[4,4],[4,2,1,1]]
+KVS = [0,0,0,0,4,4,4,5,5,5,6,6,4]
+KGS = [0,0,0,0,0,2,2,2,2,2,0,0,0]
+
+
+def tile_ufoattention_pb_kernel(tc, queries_bytes, queries_scale, Wq, bq, gamma, out):
+    nc = tc.nc
+    groups = []
+    for b in range(B):
+        j0 = 0
+        for s in SIZES[b]:
+            groups.append((b, j0, s))
+            j0 += s
+        assert j0 == TPB
+    ng = len(groups)
+    assert len(KVS) == ng
+
+    with ExitStack() as ctx:
+        const = ctx.enter_context(tc.tile_pool(name="const", bufs=1))
+        inb = ctx.enter_context(tc.tile_pool(name="inb", bufs=1))
+        xwp = ctx.enter_context(tc.tile_pool(name="xwp", bufs=3))
+        work = ctx.enter_context(tc.tile_pool(name="work", bufs=2))
+        qpool = ctx.enter_context(tc.tile_pool(name="qpool", bufs=5))
+        small = ctx.enter_context(tc.tile_pool(name="small", bufs=4))
+        ps_t = ctx.enter_context(tc.psum_pool(name="ps_t", bufs=4))
+        ps_y = ctx.enter_context(tc.psum_pool(name="ps_y", bufs=4))
+
+        scale4 = const.tile([P, SMAX * D], F32, name="scale4")
+        nc.sync.dma_start(
+            out=scale4[:, 0:D],
+            in_=queries_scale.rearrange("a b k -> (a b k)").partition_broadcast(P),
+        )
+        qbytes = []
+        for g in range(ng):
+            qb = inb.tile([P, groups[g][2] * D], U8, name="qbytes%d" % g)
+            qbytes.append(qb)
+
+        def load_bytes(g):
+            b, j0, s = groups[g]
+            nc.sync.dma_start(
+                out=qbytes[g][:],
+                in_=queries_bytes[b].rearrange("(p j) k -> p (j k)", j=TPB)[:, j0 * D : (j0 + s) * D],
+            )
+
+        load_bytes(0)
+        load_bytes(1)
+        wraw = const.tile([P, 4, D], BF16, name="wraw")
+        nc.sync.dma_start(out=wraw[:], in_=Wq.rearrange("(p j) n -> p j n", j=4))
+        load_bytes(2)
+        bias = const.tile([P, D], BF16, name="bias")
+        nc.sync.dma_start(out=bias[:], in_=bq.partition_broadcast(P))
+        load_bytes(3)
+        gam = const.tile([P, H], BF16, name="gam")
+        nc.sync.dma_start(out=gam[:], in_=gamma.rearrange("a h b c -> (a h b c)").partition_broadcast(P))
+        for g in range(4, ng):
+            load_bytes(g)
+
+        ident = const.tile([P, P], F32, name="ident")
+        make_identity(nc, ident[:])
+        one = const.tile([P, 1], F32, name="one")
+        nc.vector.memset(one[:], 1.0)
+        warm = const.tile([P, 1], F32, name="warm")
+        nc.scalar.activation(out=warm[:], in_=one[:], func=ACT.Abs_reciprocal_sqrt)
+        junk = const.tile([P, H * SMAX, DK], F32, name="junk")
+        wgrp = const.tile([P, D, 4], BF16, name="wgrp", align_bytes=64)
+        wcodes = const.tile([P, D], U32, name="wcodes", align_bytes=64)
+        wscl = const.tile([P, D], U8, name="wscl", align_bytes=64)
+
+        st = {}
+
+        def widen(g):
+            s = groups[g][2]
+            xw = xwp.tile([P, s * D], BF16, name="xw")
+            st["xw", g] = xw
+            nc.vector.tensor_tensor(out=xw[:], in0=qbytes[g][:].bitcast(FP8), in1=scale4[:, 0 : s * D], op=ALU.mult)
+
+        def chunks(s):
+            return [(j, min(2, s - j)) for j in range(0, s, 2)]
+
+        def transp(g):
+            s = groups[g][2]
+            words = st["xw", g][:].bitcast(F32)
+            for j0, n in chunks(s):
+                xt = ps_t.tile([P, n, 2, P], F32, name="xt")
+                st["xt", g, j0] = xt
+                for jj in range(n):
+                    j = j0 + jj
+                    for u in range(2):
+                        nc.tensor.transpose(xt[:, jj, u, :], words[:, 256 * j + u : 256 * (j + 1) : 2], ident[:])
+
+        def evac(g):
+            s = groups[g][2]
+            grp = work.tile([P, s * D], BF16, name="grp", align_bytes=64)
+            st["grp", g] = grp
+            gw = grp[:].bitcast(F32).rearrange("p (j r u) -> p j r u", j=s, u=2)
+            for j0, n in chunks(s):
+                nc.scalar.copy(out=gw[:, j0 : j0 + n], in_=st["xt", g, j0][:].rearrange("p j u r -> p j r u"))
+
+        def quant(g):
+            s = groups[g][2]
+            codes = work.tile([P, s * P], U32, name="codes", align_bytes=64)
+            scl = work.tile([P, s * P], U8, name="scl", align_bytes=64)
+            st["codes", g] = codes
+            st["scl", g] = scl
+            nc.vector.quantize_mx(out=codes[:].bitcast(FP8X4), scales=scl[:], in_=st["grp", g][:])
+
+        def mm(g):
+            codes = st["codes", g]
+            scl = st["scl", g]
+            for j in range(groups[g][2]):
+                y = ps_y.tile([P, D], F32, name="y")
+                st["y", g, j] = y
+                nc.tensor.matmul_mx(
+                    out=y[:],
+                    lhsT=codes[:, j * P : (j + 1) * P].bitcast(FP8X4),
+                    lhsT_scale=scl[:, j * P : (j + 1) * P],
+                    rhs=wcodes[:].bitcast(FP8X4),
+                    rhs_scale=wscl[:],
+                    start=True,
+                    stop=True,
+                )
+
+        def addb(g):
+            s = groups[g][2]
+            q = qpool.tile([P, H, s, DK], F32, name="q")
+            st["q", g] = q
+            for j in range(s):
+                nc.vector.tensor_tensor(
+                    out=q[:, :, j, :],
+                    in0=bias[:].rearrange("p (h d) -> p h d", h=H),
+                    in1=st["y", g, j][:].rearrange("p (h d) -> p h d", h=H),
+                    op=ALU.add,
+                )
+
+        def squares(g):
+            s = groups[g][2]
+            q = st["q", g]
+            ss = small.tile([P, H * s], F32, name="ss")
+            st["ss", g] = ss
+            for j in range(s):
+                for h in range(H):
+                    c = h * s + j
+                    nc.scalar.activation(out=junk[:, c, :], in_=q[:, h, j, :], func=ACT.Square, accum_out=ss[:, c : c + 1])
+
+        def rnorm(g):
+            s = groups[g][2]
+            rs = small.tile([P, H * s], F32, name="rs")
+            st["rs", g] = rs
+            nc.scalar.activation(out=rs[:], in_=st["ss", g][:], func=ACT.Abs_reciprocal_sqrt)
+
+        def gain(g):
+            s = groups[g][2]
+            rn = st["rs", g]
+            r = small.tile([P, H * s], F32, name="r")
+            st["r", g] = r
+            nc.vector.tensor_tensor(
+                out=r[:].rearrange("p (h j) -> p h j", h=H),
+                in0=rn[:].rearrange("p (h j) -> p h j", h=H),
+                in1=gam[:].unsqueeze(2).to_broadcast([P, H, s]),
+                op=ALU.mult,
+            )
+
+        def gain_g(g):
+            s = groups[g][2]
+            kv = KVS[g]
+            kg = KGS[g]
+            if kg == 0:
+                return
+            rg = small.tile([P, kg * s], F32, name="rg")
+            st["rg", g] = rg
+            nc.vector.tensor_tensor(
+                out=rg[:].rearrange("p (h j) -> p h j", h=kg),
+                in0=st["rs", g][:, kv * s : (kv + kg) * s].rearrange("p (h j) -> p h j", h=kg),
+                in1=gam[:, kv : kv + kg].unsqueeze(2).to_broadcast([P, kg, s]),
+                op=ALU.mult,
+            )
+
+        def scale_g(g):
+            s = groups[g][2]
+            kv = KVS[g]
+            kg = KGS[g]
+            if kg == 0:
+                return
+            qg = st["q", g][:, kv : kv + kg].rearrange("p h j d -> p (h j) d")
+            nc.gpsimd.tensor_tensor(
+                out=qg,
+                in0=qg,
+                in1=st["rg", g][:].unsqueeze(2).to_broadcast([P, kg * s, DK]),
+                op=ALU.mult,
+            )
+
+        def store(g, h0, h1):
+            b, j0, s = groups[g]
+            nc.sync.dma_start(
+                out=out[b].rearrange("h (p j) d -> p h (j d)", j=TPB)[:, h0:h1, j0 * DK : (j0 + s) * DK],
+                in_=st["q", g][:, h0:h1].rearrange("p h j d -> p h (j d)"),
+            )
+
+        def scale_v(g):
+            s = groups[g][2]
+            kv = KVS[g]
+            if kv == 0:
+                return
+            qv = st["q", g][:, 0:kv].rearrange("p h j d -> p (h j) d")
+            nc.vector.tensor_tensor(
+                out=qv,
+                in0=qv,
+                in1=st["r", g][:, 0 : kv * s].unsqueeze(2).to_broadcast([P, kv * s, DK]),
+                op=ALU.mult,
+            )
+            store(g, 0, kv)
+
+        def scale_s(g):
+            s = groups[g][2]
+            kv = KVS[g]
+            if kv == H:
+                return
+            q = st["q", g]
+            r = st["r", g]
+            for h in range(kv + KGS[g], H):
+                for j in range(s):
+                    c = h * s + j
+                    nc.scalar.activation(out=q[:, h, j, :], in_=q[:, h, j, :], func=ACT.Copy, scale=r[:, c : c + 1])
+            store(g, kv, H)
+
+        def ok(g):
+            return 0 <= g < ng
+
+        def spread(c0, c1):
+            nc.scalar.copy(
+                out=scale4[:, c0 * D : c1 * D].rearrange("p (c k) -> p c k", k=D),
+                in_=scale4[:, 0:D].unsqueeze(1).to_broadcast([P, c1 - c0, D]),
+            )
+
+        with tc.manual_schedule():
+            widen(0)
+            transp(0)
+            spread(1, 2)
+            widen(1)
+            transp(1)
+            evac(0)
+            nc.vector.tensor_copy(out=wgrp[:], in_=wraw[:].rearrange("p j n -> p n j"))
+            spread(2, 4)
+            nc.vector.quantize_mx(
+                out=wcodes[:].bitcast(FP8X4), scales=wscl[:], in_=wgrp[:].rearrange("p n j -> p (n j)")
+            )
+            for i in range(0, ng + 2):
+                if ok(i - 2):
+                    gain(i - 2)
+                if ok(i):
+                    quant(i)
+                    mm(i)
+                if ok(i - 1):
+                    squares(i - 1)
+                if ok(i + 2):
+                    widen(i + 2)
+                    transp(i + 2)
+                if ok(i - 2):
+                    scale_v(i - 2)
+                    gain_g(i - 2)
+                if ok(i):
+                    addb(i)
+                if ok(i - 2):
+                    scale_g(i - 2)
+                if ok(i + 1):
+                    evac(i + 1)
+                if ok(i - 1):
+                    rnorm(i - 1)
+                if ok(i - 2):
+                    scale_s(i - 2)

@@ -19,8 +19,8 @@ P = 128
 TPB = N // P
 SMAX = 4
 SIZES = [[1,1,2,2,2],[4,4],[4,4],[4,2,1,1]]
-KVS = [0,0,0,0,4,4,4,5,5,5,6,6,4]
-KGS = [0,0,0,0,0,2,2,2,2,2,0,0,0]
+KVS = [0,0,0,0,4,3,3,4,5,6,6,6,4]
+KGS = [0,0,0,0,0,3,3,3,2,1,0,0,0]
 
 
 def tile_ufoattention_pb_kernel(tc, queries_bytes, queries_scale, Wq, bq, gamma, out):

@@ -19,7 +19,7 @@ P = 128
 TPB = N // P
 SMAX = 4
 SIZES = [[1,1,2,2,2],[4,4],[4,4],[4,2,1,1]]
-KVS = [0,0,0,0,4,3,3,4,5,6,6,6,4]
+KVS = [0,0,0,0,4,4,4,5,5,6,6,6,4]
 KGS = [0,0,0,0,0,3,3,3,2,1,0,0,0]
 
 

@@ -46,10 +46,8 @@ def tile_ufoattention_pb_kernel(tc, queries_bytes, queries_scale, Wq, bq, gamma,
         ps_y = ctx.enter_context(tc.psum_pool(name="ps_y", bufs=4))
 
         scale4 = const.tile([P, SMAX * D], F32, name="scale4")
-        nc.sync.dma_start(
-            out=scale4[:, 0:D],
-            in_=queries_scale.rearrange("a b k -> (a b k)").partition_broadcast(P),
-        )
+        sc_col = const.tile([P, 4], F32, name="sc_col")
+        nc.sync.dma_start(out=sc_col[:], in_=queries_scale.rearrange("a b (c p) -> p (a b c)", p=P))
         qbytes = []
         for g in range(ng):
             qb = inb.tile([P, groups[g][2] * D], U8, name="qbytes%d" % g)
@@ -253,6 +251,10 @@ def tile_ufoattention_pb_kernel(tc, queries_bytes, queries_scale, Wq, bq, gamma,
             )
 
         with tc.manual_schedule():
+            scp = ps_y.tile([P, D], F32, name="y")
+            for c in range(4):
+                nc.tensor.transpose(scp[:, c * P : (c + 1) * P], sc_col[:, c : c + 1].to_broadcast([P, P]), ident[:])
+            nc.scalar.copy(out=scale4[:, 0:D], in_=scp[:])
             widen(0)
             transp(0)
             spread(1, 2)

@@ -60,10 +60,13 @@ def tile_ufoattention_pb_kernel(tc, queries_bytes, queries_scale, Wq, bq, gamma,
                 in_=queries_bytes[b].rearrange("(p j) k -> p (j k)", j=TPB)[:, j0 * D : (j0 + s) * D],
             )
 
+        wraw = const.tile([P, 4, D], BF16, name="wraw")
+        for c in range(2):
+            nc.sync.dma_start(
+                out=wraw[:, :, c * 256 : (c + 1) * 256], in_=Wq.rearrange("(p j) n -> p j n", j=4)[:, :, c * 256 : (c + 1) * 256]
+            )
         load_bytes(0)
         load_bytes(1)
-        wraw = const.tile([P, 4, D], BF16, name="wraw")
-        nc.sync.dma_start(out=wraw[:], in_=Wq.rearrange("(p j) n -> p j n", j=4))
         load_bytes(2)
         bias = const.tile([P, D], BF16, name="bias")
         nc.sync.dma_start(out=bias[:], in_=bq.partition_broadcast(P))
@@ -255,17 +258,20 @@ def tile_ufoattention_pb_kernel(tc, queries_bytes, queries_scale, Wq, bq, gamma,
             for c in range(4):
                 nc.tensor.transpose(scp[:, c * P : (c + 1) * P], sc_col[:, c : c + 1].to_broadcast([P, P]), ident[:])
             nc.scalar.copy(out=scale4[:, 0:D], in_=scp[:])
+            for c in range(2):
+                nc.vector.tensor_copy(
+                    out=wgrp[:, c * 256 : (c + 1) * 256, :], in_=wraw[:, :, c * 256 : (c + 1) * 256].rearrange("p j n -> p n j")
+                )
             widen(0)
             transp(0)
             spread(1, 2)
-            widen(1)
-            transp(1)
-            evac(0)
-            nc.vector.tensor_copy(out=wgrp[:], in_=wraw[:].rearrange("p j n -> p n j"))
-            spread(2, 4)
             nc.vector.quantize_mx(
                 out=wcodes[:].bitcast(FP8X4), scales=wscl[:], in_=wgrp[:].rearrange("p n j -> p (n j)")
             )
+            widen(1)
+            transp(1)
+            evac(0)
+            spread(2, 4)
             for i in range(0, ng + 2):
                 if ok(i - 2):
                     gain(i - 2)

@@ -18,9 +18,9 @@ ACT = mybir.ActivationFunctionType
 P = 128
 TPB = N // P
 SMAX = 4
-SIZES = [[1,1,2,2,2],[4,4],[4,4],[4,2,1,1]]
-KVS = [0,0,0,0,4,4,4,5,5,6,6,6,4]
-KGS = [0,0,0,0,0,3,3,3,2,1,0,0,0]
+SIZES = [[1,1,2,2,2],[4,4],[4,4],[4,2,2]]
+KVS = [0,0,0,0,4,4,4,5,5,6,6,4]
+KGS = [0,0,0,0,0,3,3,3,2,2,0,0]
 
 
 def tile_ufoattention_pb_kernel(tc, queries_bytes, queries_scale, Wq, bq, gamma, out):
@@ -47,7 +47,7 @@ def tile_ufoattention_pb_kernel(tc, queries_bytes, queries_scale, Wq, bq, gamma,
 
         scale4 = const.tile([P, SMAX * D], F32, name="scale4")
         sc_col = const.tile([P, 4], F32, name="sc_col")
-        nc.sync.dma_start(out=sc_col[:], in_=queries_scale.rearrange("a b (c p) -> p (a b c)", p=P))
+        nc.sync.dma_start(out=sc_col[:], in_=queries_scale.rearrange("a b (p c) -> p (a b c)", c=4))
         qbytes = []
         for g in range(ng):
             qb = inb.tile([P, groups[g][2] * D], U8, name="qbytes%d" % g)
@@ -257,7 +257,9 @@ def tile_ufoattention_pb_kernel(tc, queries_bytes, queries_scale, Wq, bq, gamma,
             scp = ps_y.tile([P, D], F32, name="y")
             for c in range(4):
                 nc.tensor.transpose(scp[:, c * P : (c + 1) * P], sc_col[:, c : c + 1].to_broadcast([P, P]), ident[:])
-            nc.scalar.copy(out=scale4[:, 0:D], in_=scp[:])
+            nc.scalar.copy(
+                out=scale4[:, 0:D].rearrange("q (p c) -> q p c", c=4), in_=scp[:].rearrange("q (c p) -> q p c", c=4)
+            )
             for c in range(2):
                 nc.vector.tensor_copy(
                     out=wgrp[:, c * 256 : (c + 1) * 256, :], in_=wraw[:, :, c * 256 : (c + 1) * 256].rearrange("p j n -> p n j")

@@ -19,8 +19,9 @@ P = 128
 TPB = N // P
 SMAX = 4
 SIZES = [[1,1,2,2,2],[4,4],[4,4],[4,2,2]]
-KVS = [0,0,0,0,4,4,4,5,5,6,6,4]
-KGS = [0,0,0,0,0,3,3,3,2,2,0,0]
+KVS = [0,0,0,0,1,1,1,1,2,3,5,4]
+CAST = "gggggggggggg"
+KGS = [0,0,0,0,2,3,3,3,2,2,0,0]
 
 
 def tile_ufoattention_pb_kernel(tc, queries_bytes, queries_scale, Wq, bq, gamma, out):
@@ -45,7 +46,6 @@ def tile_ufoattention_pb_kernel(tc, queries_bytes, queries_scale, Wq, bq, gamma,
         ps_t = ctx.enter_context(tc.psum_pool(name="ps_t", bufs=4))
         ps_y = ctx.enter_context(tc.psum_pool(name="ps_y", bufs=4))
 
-        scale4 = const.tile([P, SMAX * D], F32, name="scale4")
         sc_col = const.tile([P, 4], F32, name="sc_col")
         nc.sync.dma_start(out=sc_col[:], in_=queries_scale.rearrange("a b (p c) -> p (a b c)", c=4))
         qbytes = []
@@ -89,11 +89,14 @@ def tile_ufoattention_pb_kernel(tc, queries_bytes, queries_scale, Wq, bq, gamma,
 
         st = {}
 
-        def widen(g):
+        def cast(g):
             s = groups[g][2]
             xw = xwp.tile([P, s * D], BF16, name="xw")
             st["xw", g] = xw
-            nc.vector.tensor_tensor(out=xw[:], in0=qbytes[g][:].bitcast(FP8), in1=scale4[:, 0 : s * D], op=ALU.mult)
+            if CAST[g] == "s":
+                nc.scalar.copy(out=xw[:], in_=qbytes[g][:].bitcast(FP8))
+            else:
+                nc.gpsimd.tensor_copy(out=xw[:], in_=qbytes[g][:].bitcast(FP8))
 
         def chunks(s):
             return [(j, min(2, s - j)) for j in range(0, s, 2)]
@@ -102,20 +105,24 @@ def tile_ufoattention_pb_kernel(tc, queries_bytes, queries_scale, Wq, bq, gamma,
             s = groups[g][2]
             words = st["xw", g][:].bitcast(F32)
             for j0, n in chunks(s):
-                xt = ps_t.tile([P, n, 2, P], F32, name="xt")
+                xt = ps_t.tile([P, 2, n * P], F32, name="xt")
                 st["xt", g, j0] = xt
                 for jj in range(n):
                     j = j0 + jj
                     for u in range(2):
-                        nc.tensor.transpose(xt[:, jj, u, :], words[:, 256 * j + u : 256 * (j + 1) : 2], ident[:])
+                        nc.tensor.transpose(xt[:, u, jj * P : (jj + 1) * P], words[:, 256 * j + u : 256 * (j + 1) : 2], ident[:])
 
         def evac(g):
             s = groups[g][2]
             grp = work.tile([P, s * D], BF16, name="grp", align_bytes=64)
             st["grp", g] = grp
-            gw = grp[:].bitcast(F32).rearrange("p (j r u) -> p j r u", j=s, u=2)
             for j0, n in chunks(s):
-                nc.scalar.copy(out=gw[:, j0 : j0 + n], in_=st["xt", g, j0][:].rearrange("p j u r -> p j r u"))
+                nc.vector.tensor_tensor(
+                    out=grp[:, j0 * D : (j0 + n) * D].rearrange("p (x u e) -> p x u e", u=2, e=2),
+                    in0=st["xt", g, j0][:].bitcast(BF16).rearrange("p u (x e) -> p x u e", e=2),
+                    in1=sc_col[:].rearrange("p (u e) -> p u e", e=2).unsqueeze(1).to_broadcast([P, n * P, 2, 2]),
+                    op=ALU.mult,
+                )
 
         def quant(g):
             s = groups[g][2]
@@ -247,33 +254,20 @@ def tile_ufoattention_pb_kernel(tc, queries_bytes, queries_scale, Wq, bq, gamma,
         def ok(g):
             return 0 <= g < ng
 
-        def spread(c0, c1):
-            nc.scalar.copy(
-                out=scale4[:, c0 * D : c1 * D].rearrange("p (c k) -> p c k", k=D),
-                in_=scale4[:, 0:D].unsqueeze(1).to_broadcast([P, c1 - c0, D]),
-            )
-
         with tc.manual_schedule():
-            scp = ps_y.tile([P, D], F32, name="y")
-            for c in range(4):
-                nc.tensor.transpose(scp[:, c * P : (c + 1) * P], sc_col[:, c : c + 1].to_broadcast([P, P]), ident[:])
-            nc.scalar.copy(
-                out=scale4[:, 0:D].rearrange("q (p c) -> q p c", c=4), in_=scp[:].rearrange("q (c p) -> q p c", c=4)
-            )
+            cast(0)
+            transp(0)
+            cast(1)
+            transp(1)
+            cast(2)
             for c in range(2):
                 nc.vector.tensor_copy(
                     out=wgrp[:, c * 256 : (c + 1) * 256, :], in_=wraw[:, :, c * 256 : (c + 1) * 256].rearrange("p j n -> p n j")
                 )
-            widen(0)
-            transp(0)
-            spread(1, 2)
             nc.vector.quantize_mx(
                 out=wcodes[:].bitcast(FP8X4), scales=wscl[:], in_=wgrp[:].rearrange("p n j -> p (n j)")
             )
-            widen(1)
-            transp(1)
             evac(0)
-            spread(2, 4)
             for i in range(0, ng + 2):
                 if ok(i - 2):
                     gain(i - 2)
@@ -283,18 +277,19 @@ def tile_ufoattention_pb_kernel(tc, queries_bytes, queries_scale, Wq, bq, gamma,
                 if ok(i - 1):
                     squares(i - 1)
                 if ok(i + 2):
-                    widen(i + 2)
                     transp(i + 2)
                 if ok(i - 2):
                     scale_v(i - 2)
                     gain_g(i - 2)
+                if ok(i + 1):
+                    evac(i + 1)
                 if ok(i):
                     addb(i)
                 if ok(i - 2):
                     scale_g(i - 2)
-                if ok(i + 1):
-                    evac(i + 1)
                 if ok(i - 1):
                     rnorm(i - 1)
                 if ok(i - 2):
                     scale_s(i - 2)
+                if ok(i + 3):
+                    cast(i + 3)

@@ -19,9 +19,9 @@ P = 128
 TPB = N // P
 SMAX = 4
 SIZES = [[1,1,2,2,2],[4,4],[4,4],[4,2,2]]
-KVS = [0,0,0,0,1,1,1,1,2,3,5,4]
-CAST = "gggggggggggg"
-KGS = [0,0,0,0,2,3,3,3,2,2,0,0]
+KVS = [0,0,0,0,0,0,0,1,3,5,7,3]
+CAST = "sssssggggggg"
+KGS = [0,0,0,0,0,5,5,5,3,1,0,0]
 
 
 def tile_ufoattention_pb_kernel(tc, queries_bytes, queries_scale, Wq, bq, gamma, out):
@@ -39,7 +39,7 @@ def tile_ufoattention_pb_kernel(tc, queries_bytes, queries_scale, Wq, bq, gamma,
     with ExitStack() as ctx:
         const = ctx.enter_context(tc.tile_pool(name="const", bufs=1))
         inb = ctx.enter_context(tc.tile_pool(name="inb", bufs=1))
-        xwp = ctx.enter_context(tc.tile_pool(name="xwp", bufs=3))
+        xwp = ctx.enter_context(tc.tile_pool(name="xwp", bufs=4))
         work = ctx.enter_context(tc.tile_pool(name="work", bufs=2))
         qpool = ctx.enter_context(tc.tile_pool(name="qpool", bufs=5))
         small = ctx.enter_context(tc.tile_pool(name="small", bufs=4))
@@ -60,12 +60,12 @@ def tile_ufoattention_pb_kernel(tc, queries_bytes, queries_scale, Wq, bq, gamma,
                 in_=queries_bytes[b].rearrange("(p j) k -> p (j k)", j=TPB)[:, j0 * D : (j0 + s) * D],
             )
 
+        load_bytes(0)
         wraw = const.tile([P, 4, D], BF16, name="wraw")
         for c in range(2):
             nc.sync.dma_start(
                 out=wraw[:, :, c * 256 : (c + 1) * 256], in_=Wq.rearrange("(p j) n -> p j n", j=4)[:, :, c * 256 : (c + 1) * 256]
             )
-        load_bytes(0)
         load_bytes(1)
         load_bytes(2)
         bias = const.tile([P, D], BF16, name="bias")
@@ -260,6 +260,9 @@ def tile_ufoattention_pb_kernel(tc, queries_bytes, queries_scale, Wq, bq, gamma,
             cast(1)
             transp(1)
             cast(2)
+            cast(3)
+            cast(4)
+            cast(5)
             for c in range(2):
                 nc.vector.tensor_copy(
                     out=wgrp[:, c * 256 : (c + 1) * 256, :], in_=wraw[:, :, c * 256 : (c + 1) * 256].rearrange("p j n -> p n j")
@@ -269,11 +272,11 @@ def tile_ufoattention_pb_kernel(tc, queries_bytes, queries_scale, Wq, bq, gamma,
             )
             evac(0)
             for i in range(0, ng + 2):
-                if ok(i - 2):
-                    gain(i - 2)
                 if ok(i):
                     quant(i)
                     mm(i)
+                if ok(i - 2):
+                    gain(i - 2)
                 if ok(i - 1):
                     squares(i - 1)
                 if ok(i + 2):
@@ -287,9 +290,9 @@ def tile_ufoattention_pb_kernel(tc, queries_bytes, queries_scale, Wq, bq, gamma,
                     addb(i)
                 if ok(i - 2):
                     scale_g(i - 2)
-                if ok(i - 1):
-                    rnorm(i - 1)
                 if ok(i - 2):
                     scale_s(i - 2)
-                if ok(i + 3):
-                    cast(i + 3)
+                if ok(i - 1):
+                    rnorm(i - 1)
+                if i >= 2 and ok(i + 4):
+                    cast(i + 4)

@@ -19,9 +19,9 @@ P = 128
 TPB = N // P
 SMAX = 4
 SIZES = [[1,1,2,2,2],[4,4],[4,4],[4,2,2]]
-KVS = [0,0,0,0,0,0,0,1,3,5,7,3]
+KVS = [0,0,0,0,0,0,0,1,3,4,5,3]
 CAST = "sssssggggggg"
-KGS = [0,0,0,0,0,5,5,5,3,1,0,0]
+KGS = [0,0,2,0,5,6,7,6,5,3,2,0]
 
 
 def tile_ufoattention_pb_kernel(tc, queries_bytes, queries_scale, Wq, bq, gamma, out):
@@ -188,21 +188,6 @@ def tile_ufoattention_pb_kernel(tc, queries_bytes, queries_scale, Wq, bq, gamma,
                 op=ALU.mult,
             )
 
-        def gain_g(g):
-            s = groups[g][2]
-            kv = KVS[g]
-            kg = KGS[g]
-            if kg == 0:
-                return
-            rg = small.tile([P, kg * s], F32, name="rg")
-            st["rg", g] = rg
-            nc.vector.tensor_tensor(
-                out=rg[:].rearrange("p (h j) -> p h j", h=kg),
-                in0=st["rs", g][:, kv * s : (kv + kg) * s].rearrange("p (h j) -> p h j", h=kg),
-                in1=gam[:, kv : kv + kg].unsqueeze(2).to_broadcast([P, kg, s]),
-                op=ALU.mult,
-            )
-
         def scale_g(g):
             s = groups[g][2]
             kv = KVS[g]
@@ -213,7 +198,7 @@ def tile_ufoattention_pb_kernel(tc, queries_bytes, queries_scale, Wq, bq, gamma,
             nc.gpsimd.tensor_tensor(
                 out=qg,
                 in0=qg,
-                in1=st["rg", g][:].unsqueeze(2).to_broadcast([P, kg * s, DK]),
+                in1=st["r", g][:, kv * s : (kv + kg) * s].unsqueeze(2).to_broadcast([P, kg * s, DK]),
                 op=ALU.mult,
             )
 
@@ -283,7 +268,6 @@ def tile_ufoattention_pb_kernel(tc, queries_bytes, queries_scale, Wq, bq, gamma,
                     transp(i + 2)
                 if ok(i - 2):
                     scale_v(i - 2)
-                    gain_g(i - 2)
                 if ok(i + 1):
                     evac(i + 1)
                 if ok(i):

from contextlib import ExitStack

import concourse.mybir as mybir
from concourse.masks import make_identity

B, N, D, H, DK = 4, 1024, 512, 8, 64
FLOPS = 2 * B * N * D * H * DK

F32 = mybir.dt.float32
BF16 = mybir.dt.bfloat16
U32 = mybir.dt.uint32
U8 = mybir.dt.uint8
FP8 = mybir.dt.float8_e4m3fn
FP8X4 = mybir.dt.float8_e4m3fn_x4
ALU = mybir.AluOpType
ACT = mybir.ActivationFunctionType

P = 128
TPB = N // P
SMAX = 4
SIZES = [[1,1,2,2,2],[4,4],[4,4],[4,2,2]]
KVS = [0,0,0,0,0,0,0,1,3,4,5,3]
CAST = "sssssggggggg"
KGS = [0,0,2,0,5,6,7,6,5,3,2,0]


def tile_ufoattention_pb_kernel(tc, queries_bytes, queries_scale, Wq, bq, gamma, out):
    nc = tc.nc
    groups = []
    for b in range(B):
        j0 = 0
        for s in SIZES[b]:
            groups.append((b, j0, s))
            j0 += s
        assert j0 == TPB
    ng = len(groups)
    assert len(KVS) == ng

    with ExitStack() as ctx:
        const = ctx.enter_context(tc.tile_pool(name="const", bufs=1))
        inb = ctx.enter_context(tc.tile_pool(name="inb", bufs=1))
        xwp = ctx.enter_context(tc.tile_pool(name="xwp", bufs=4))
        work = ctx.enter_context(tc.tile_pool(name="work", bufs=2))
        qpool = ctx.enter_context(tc.tile_pool(name="qpool", bufs=5))
        small = ctx.enter_context(tc.tile_pool(name="small", bufs=4))
        ps_t = ctx.enter_context(tc.psum_pool(name="ps_t", bufs=4))
        ps_y = ctx.enter_context(tc.psum_pool(name="ps_y", bufs=4))

        sc_col = const.tile([P, 4], F32, name="sc_col")
        nc.sync.dma_start(out=sc_col[:], in_=queries_scale.rearrange("a b (p c) -> p (a b c)", c=4))
        qbytes = []
        for g in range(ng):
            qb = inb.tile([P, groups[g][2] * D], U8, name="qbytes%d" % g)
            qbytes.append(qb)

        def load_bytes(g):
            b, j0, s = groups[g]
            nc.sync.dma_start(
                out=qbytes[g][:],
                in_=queries_bytes[b].rearrange("(p j) k -> p (j k)", j=TPB)[:, j0 * D : (j0 + s) * D],
            )

        load_bytes(0)
        wraw = const.tile([P, 4, D], BF16, name="wraw")
        for c in range(2):
            nc.sync.dma_start(
                out=wraw[:, :, c * 256 : (c + 1) * 256], in_=Wq.rearrange("(p j) n -> p j n", j=4)[:, :, c * 256 : (c + 1) * 256]
            )
        load_bytes(1)
        load_bytes(2)
        bias = const.tile([P, D], BF16, name="bias")
        nc.sync.dma_start(out=bias[:], in_=bq.partition_broadcast(P))
        load_bytes(3)
        gam = const.tile([P, H], BF16, name="gam")
        nc.sync.dma_start(out=gam[:], in_=gamma.rearrange("a h b c -> (a h b c)").partition_broadcast(P))
        for g in range(4, ng):
            load_bytes(g)

        ident = const.tile([P, P], F32, name="ident")
        make_identity(nc, ident[:])
        one = const.tile([P, 1], F32, name="one")
        nc.vector.memset(one[:], 1.0)
        warm = const.tile([P, 1], F32, name="warm")
        nc.scalar.activation(out=warm[:], in_=one[:], func=ACT.Abs_reciprocal_sqrt)
        junk = const.tile([P, H * SMAX, DK], F32, name="junk")
        wgrp = const.tile([P, D, 4], BF16, name="wgrp", align_bytes=64)
        wcodes = const.tile([P, D], U32, name="wcodes", align_bytes=64)
        wscl = const.tile([P, D], U8, name="wscl", align_bytes=64)

        st = {}

        def cast(g):
            s = groups[g][2]
            xw = xwp.tile([P, s * D], BF16, name="xw")
            st["xw", g] = xw
            if CAST[g] == "s":
                nc.scalar.copy(out=xw[:], in_=qbytes[g][:].bitcast(FP8))
            else:
                nc.gpsimd.tensor_copy(out=xw[:], in_=qbytes[g][:].bitcast(FP8))

        def chunks(s):
            return [(j, min(2, s - j)) for j in range(0, s, 2)]

        def transp(g):
            s = groups[g][2]
            words = st["xw", g][:].bitcast(F32)
            for j0, n in chunks(s):
                xt = ps_t.tile([P, 2, n * P], F32, name="xt")
                st["xt", g, j0] = xt
                for jj in range(n):
                    j = j0 + jj
                    for u in range(2):
                        nc.tensor.transpose(xt[:, u, jj * P : (jj + 1) * P], words[:, 256 * j + u : 256 * (j + 1) : 2], ident[:])

        def evac(g):
            s = groups[g][2]
            grp = work.tile([P, s * D], BF16, name="grp", align_bytes=64)
            st["grp", g] = grp
            for j0, n in chunks(s):
                nc.vector.tensor_tensor(
                    out=grp[:, j0 * D : (j0 + n) * D].rearrange("p (x u e) -> p x u e", u=2, e=2),
                    in0=st["xt", g, j0][:].bitcast(BF16).rearrange("p u (x e) -> p x u e", e=2),
                    in1=sc_col[:].rearrange("p (u e) -> p u e", e=2).unsqueeze(1).to_broadcast([P, n * P, 2, 2]),
                    op=ALU.mult,
                )

        def quant(g):
            s = groups[g][2]
            codes = work.tile([P, s * P], U32, name="codes", align_bytes=64)
            scl = work.tile([P, s * P], U8, name="scl", align_bytes=64)
            st["codes", g] = codes
            st["scl", g] = scl
            nc.vector.quantize_mx(out=codes[:].bitcast(FP8X4), scales=scl[:], in_=st["grp", g][:])

        def mm(g):
            codes = st["codes", g]
            scl = st["scl", g]
            for j in range(groups[g][2]):
                y = ps_y.tile([P, D], F32, name="y")
                st["y", g, j] = y
                nc.tensor.matmul_mx(
                    out=y[:],
                    lhsT=codes[:, j * P : (j + 1) * P].bitcast(FP8X4),
                    lhsT_scale=scl[:, j * P : (j + 1) * P],
                    rhs=wcodes[:].bitcast(FP8X4),
                    rhs_scale=wscl[:],
                    start=True,
                    stop=True,
                )

        def addb(g):
            s = groups[g][2]
            q = qpool.tile([P, H, s, DK], F32, name="q")
            st["q", g] = q
            for j in range(s):
                nc.vector.tensor_tensor(
                    out=q[:, :, j, :],
                    in0=bias[:].rearrange("p (h d) -> p h d", h=H),
                    in1=st["y", g, j][:].rearrange("p (h d) -> p h d", h=H),
                    op=ALU.add,
                )

        def squares(g):
            s = groups[g][2]
            q = st["q", g]
            ss = small.tile([P, H * s], F32, name="ss")
            st["ss", g] = ss
            for j in range(s):
                for h in range(H):
                    c = h * s + j
                    nc.scalar.activation(out=junk[:, c, :], in_=q[:, h, j, :], func=ACT.Square, accum_out=ss[:, c : c + 1])

        def rnorm(g):
            s = groups[g][2]
            rs = small.tile([P, H * s], F32, name="rs")
            st["rs", g] = rs
            nc.scalar.activation(out=rs[:], in_=st["ss", g][:], func=ACT.Abs_reciprocal_sqrt)

        def gain(g):
            s = groups[g][2]
            rn = st["rs", g]
            r = small.tile([P, H * s], F32, name="r")
            st["r", g] = r
            nc.vector.tensor_tensor(
                out=r[:].rearrange("p (h j) -> p h j", h=H),
                in0=rn[:].rearrange("p (h j) -> p h j", h=H),
                in1=gam[:].unsqueeze(2).to_broadcast([P, H, s]),
                op=ALU.mult,
            )

        def scale_g(g):
            s = groups[g][2]
            kv = KVS[g]
            kg = KGS[g]
            if kg == 0:
                return
            qg = st["q", g][:, kv : kv + kg].rearrange("p h j d -> p (h j) d")
            nc.gpsimd.tensor_tensor(
                out=qg,
                in0=qg,
                in1=st["r", g][:, kv * s : (kv + kg) * s].unsqueeze(2).to_broadcast([P, kg * s, DK]),
                op=ALU.mult,
            )

        def store(g, h0, h1):
            b, j0, s = groups[g]
            nc.sync.dma_start(
                out=out[b].rearrange("h (p j) d -> p h (j d)", j=TPB)[:, h0:h1, j0 * DK : (j0 + s) * DK],
                in_=st["q", g][:, h0:h1].rearrange("p h j d -> p h (j d)"),
            )

        def scale_v(g):
            s = groups[g][2]
            kv = KVS[g]
            if kv == 0:
                return
            qv = st["q", g][:, 0:kv].rearrange("p h j d -> p (h j) d")
            nc.vector.tensor_tensor(
                out=qv,
                in0=qv,
                in1=st["r", g][:, 0 : kv * s].unsqueeze(2).to_broadcast([P, kv * s, DK]),
                op=ALU.mult,
            )
            store(g, 0, kv)

        def scale_s(g):
            s = groups[g][2]
            kv = KVS[g]
            if kv == H:
                return
            q = st["q", g]
            r = st["r", g]
            for h in range(kv + KGS[g], H):
                for j in range(s):
                    c = h * s + j
                    nc.scalar.activation(out=q[:, h, j, :], in_=q[:, h, j, :], func=ACT.Copy, scale=r[:, c : c + 1])
            store(g, kv, H)

        def ok(g):
            return 0 <= g < ng

        with tc.manual_schedule():
            cast(0)
            transp(0)
            cast(1)
            transp(1)
            cast(2)
            cast(3)
            cast(4)
            cast(5)
            for c in range(2):
                nc.vector.tensor_copy(
                    out=wgrp[:, c * 256 : (c + 1) * 256, :], in_=wraw[:, :, c * 256 : (c + 1) * 256].rearrange("p j n -> p n j")
                )
            nc.vector.quantize_mx(
                out=wcodes[:].bitcast(FP8X4), scales=wscl[:], in_=wgrp[:].rearrange("p n j -> p (n j)")
            )
            evac(0)
            for i in range(0, ng + 2):
                if ok(i):
                    quant(i)
                    mm(i)
                if ok(i - 2):
                    gain(i - 2)
                if ok(i - 1):
                    squares(i - 1)
                if ok(i + 2):
                    transp(i + 2)
                if ok(i - 2):
                    scale_v(i - 2)
                if ok(i + 1):
                    evac(i + 1)
                if ok(i):
                    addb(i)
                if ok(i - 2):
                    scale_g(i - 2)
                if ok(i - 2):
                    scale_s(i - 2)
                if ok(i - 1):
                    rnorm(i - 1)
                if i >= 2 and ok(i + 4):
                    cast(i + 4)
